import numpy as np
import ml_dtypes


def mxq(x, axis, fmt="e4m3"):
    dtype, down = {"e4m3": (ml_dtypes.float8_e4m3fn, 7), "e5m2": (ml_dtypes.float8_e5m2, 14)}[fmt]
    v = np.moveaxis(np.asarray(x, np.float32).astype(ml_dtypes.bfloat16).astype(np.float64), axis, -1)
    blocks = v.reshape(v.shape[:-1] + (-1, 32))
    amax = np.abs(blocks).max(-1, keepdims=True)
    byte = np.maximum(np.where(amax > 0, np.frexp(amax)[1] - 1 + 127, 0) - down, 1)
    scale = np.exp2(byte - 127.0)
    codes = (blocks / scale).astype(np.float32).astype(dtype).astype(np.float64)
    return np.moveaxis((codes * scale).reshape(v.shape), -1, axis)


WIDE = False


def mx_kscale(k):
    if not WIDE:
        return np.ones(k)
    levels = np.array([10, -10, 5, -5, 0])
    if k % 512:
        return np.exp2(np.random.permutation(np.resize(levels, k // 32))).repeat(32)
    a = np.empty((k // 512, 16))
    for p in range(k // 512):
        a[p, :8] = np.random.permutation(np.resize(levels, 8))
        for g in range(8):
            far = levels[np.abs(levels - a[p, g]) >= 10]
            a[p, g + 8] = far[np.random.randint(len(far))]
    return np.exp2(a.ravel()).repeat(32)


BF16 = ml_dtypes.bfloat16


def bf(x):
    return np.asarray(x, np.float32).astype(BF16)


def f64(x):
    return np.asarray(x).astype(np.float64)


B, N, D, P, Z = 8, 512, 1024, 511, 2
P1 = P + 1


def leaky_draw(shape):
    g = np.random.standard_normal(shape)
    return np.where(g > 0.0, g, 0.1 * g)


def with_ones(v):
    return np.concatenate([v, np.ones(v.shape[:-1] + (1,))], axis=-1)


def setup_inputs():
    s, u = mx_kscale(P1), mx_kscale(P1)
    s, u = s / s[-1], u / u[-1]
    return {"xp": bf(leaky_draw((B, N, P)) * s[:P]),
            "yp": bf(leaky_draw((B, N, P)) / u[:P]),
            "w": bf(np.random.standard_normal((B, Z, P1, P1)) * 0.36 / np.sqrt(P1) / s[:, None] * u)}


def reference(xp, yp, w):
    x1 = mxq(with_ones(f64(xp)), 2, "e4m3")
    y1 = mxq(with_ones(f64(yp)), 2, "e4m3")
    t = x1[:, None] @ mxq(f64(w), 2, "e4m3")
    sc = mxq(t, 3, "e4m3") @ y1.transpose(0, 2, 1)[:, None]
    return sc.transpose(0, 2, 3, 1)

@@ -1,0 +1,172 @@
+from contextlib import ExitStack
+
+import concourse.mybir as mybir
+from concourse.masks import make_identity
+
+BF16 = mybir.dt.bfloat16
+F32 = mybir.dt.float32
+U32 = mybir.dt.uint32
+U8 = mybir.dt.uint8
+FP8X4 = mybir.dt.float8_e4m3fn_x4
+
+B = 8
+Z = 2
+N = 512
+K = 512
+P = 128
+PACK = 4
+ROWS = N // P
+HALF = N // 2
+
+UNITS = B * ROWS
+RAW_SLOTS = 4
+RESULT_SLOTS = 16
+PREP_LEAD = 6
+STAGE1_LEAD = 2
+
+FLOPS = 2 * 2 * B * Z * N * K * K
+
+
+def tile_span2oscorer_pa_t_kernel(tc, xp, yp, w, out):
+    nc = tc.nc
+    with ExitStack() as stack:
+        fixed = stack.enter_context(tc.tile_pool(name="fixed", bufs=1))
+        grouped = stack.enter_context(tc.tile_pool(name="grouped", bufs=3))
+        results = stack.enter_context(tc.tile_pool(name="results", bufs=RESULT_SLOTS))
+        flip_banks = stack.enter_context(tc.psum_pool(name="flip_banks", bufs=2))
+        t_banks = stack.enter_context(tc.psum_pool(name="t_banks", bufs=3))
+        out_banks = stack.enter_context(tc.psum_pool(name="out_banks", bufs=3))
+        stack.enter_context(tc.manual_schedule())
+
+        identity = fixed.tile([P, P], F32)
+        make_identity(nc, identity[:])
+
+        x_raw = fixed.tile([P, RAW_SLOTS, ROWS, K], BF16)
+        y_raw = fixed.tile([P, RAW_SLOTS, ROWS, K], BF16)
+        w_raw = fixed.tile([P, RAW_SLOTS, Z, PACK, K], BF16)
+        nc.vector.memset(x_raw[:, :, :, K - 16 : K], 1.0)
+        nc.vector.memset(y_raw[:, :, :, K - 16 : K], 1.0)
+
+        x_codes = fixed.tile([P, 2, N], U32, align_bytes=64)
+        x_scales = fixed.tile([P, 2, N], U8, align_bytes=64)
+        y_codes = fixed.tile([P, 2, N], U32, align_bytes=64)
+        y_scales = fixed.tile([P, 2, N], U8, align_bytes=64)
+        w_codes = fixed.tile([P, 2, Z, K], U32, align_bytes=64)
+        w_scales = fixed.tile([P, 2, Z, K], U8, align_bytes=64)
+
+        def load(b):
+            slot = b % RAW_SLOTS
+            for z in range(Z):
+                nc.sync.dma_start(
+                    out=w_raw[:, slot, z], in_=w[b, z].rearrange("(p t) j -> p t j", t=PACK)
+                )
+                if z == 0:
+                    nc.sync.dma_start(
+                        out=x_raw[:, slot, :, 0 : K - 1], in_=xp[b].rearrange("(m r) k -> m r k", r=ROWS)
+                    )
+            nc.sync.dma_start(out=y_raw[:, slot, :, 0 : K - 1], in_=yp[b].rearrange("(r m) k -> m r k", r=ROWS))
+
+        def prepare(piece):
+            b, quarter = divmod(piece, ROWS)
+            slot, parity = b % RAW_SLOTS, b % 2
+            first, half = divmod(quarter, 2)
+            cols = slice(half * HALF, (half + 1) * HALF)
+
+            raw, codes, scales = ((x_raw, x_codes, x_scales), (y_raw, y_codes, y_scales))[first]
+            words = raw[:, slot].bitcast(F32)
+            flipped = flip_banks.tile([P, 2, 2, P], F32)
+            for pair_row in range(2):
+                for u in range(2):
+                    nc.tensor.transpose(
+                        flipped[:, pair_row, u, :], words[:, 2 * half + pair_row, u::2], identity[:]
+                    )
+            xy_grouped = grouped.tile([P, 2, P, PACK], BF16, align_bytes=64)
+            nc.scalar.copy(out=xy_grouped[:].bitcast(F32), in_=flipped[:].rearrange("p r u m -> p r m u"))
+
+            w_grouped = grouped.tile([P, 2, P, PACK], BF16, align_bytes=64)
+            nc.vector.tensor_copy(
+                out=w_grouped[:],
+                in_=w_raw[:, slot, first].rearrange("p t (q f) -> p f q t", f=PACK)[:, 2 * half : 2 * half + 2],
+            )
+            nc.vector.quantize_mx(
+                out=codes[:, parity, cols].bitcast(FP8X4),
+                scales=scales[:, parity, cols],
+                in_=xy_grouped[:].rearrange("p r m t -> p (r m t)"),
+            )
+            nc.vector.quantize_mx(
+                out=w_codes[:, parity, first, cols].bitcast(FP8X4),
+                scales=w_scales[:, parity, first, cols],
+                in_=w_grouped[:].rearrange("p f q t -> p (f q t)"),
+            )
+            if quarter == ROWS - 1 and b + RAW_SLOTS < B:
+                load(b + RAW_SLOTS)
+
+        t_grouped = {}
+        t_quantised = {}
+
+        def stage1(unit):
+            b, r = divmod(unit, ROWS)
+            parity = b % 2
+            t_grouped[unit] = grouped.tile([P, Z, P, PACK], BF16, align_bytes=64, name="t_grouped")
+            for z in range(Z):
+                t_bank = t_banks.tile([P, PACK, P], F32)
+                for t in range(PACK):
+                    nc.tensor.matmul_mx(
+                        out=t_bank[:, t, :],
+                        lhsT=w_codes[:, parity, z, t * P : (t + 1) * P].bitcast(FP8X4),
+                        lhsT_scale=w_scales[:, parity, z, t * P : (t + 1) * P],
+                        rhs=x_codes[:, parity, r * P : (r + 1) * P].bitcast(FP8X4),
+                        rhs_scale=x_scales[:, parity, r * P : (r + 1) * P],
+                        start=True,
+                        stop=True,
+                    )
+                nc.scalar.copy(out=t_grouped[unit][:, z], in_=t_bank[:].rearrange("p t m -> p m t"))
+
+        def quantise_t(unit):
+            t_codes = grouped.tile([P, Z * P], U32, align_bytes=64)
+            t_scales = grouped.tile([P, Z * P], U8, align_bytes=64)
+            nc.vector.quantize_mx(
+                out=t_codes[:].bitcast(FP8X4),
+                scales=t_scales[:],
+                in_=t_grouped[unit][:].rearrange("p z m t -> p (z m t)"),
+            )
+            t_quantised[unit] = (t_codes, t_scales)
+
+        def stage2(unit):
+            b, r = divmod(unit, ROWS)
+            parity = b % 2
+            t_codes, t_scales = t_quantised[unit]
+            result = results.tile([P, N, Z], F32)
+            for half in range(2):
+                cols = slice(half * HALF, (half + 1) * HALF)
+                out_bank = out_banks.tile([P, Z, HALF], F32)
+                for z in range(Z):
+                    nc.tensor.matmul_mx(
+                        out=out_bank[:, z, :],
+                        lhsT=t_codes[:, z * P : (z + 1) * P].bitcast(FP8X4),
+                        lhsT_scale=t_scales[:, z * P : (z + 1) * P],
+                        rhs=y_codes[:, parity, cols].bitcast(FP8X4),
+                        rhs_scale=y_scales[:, parity, cols],
+                        start=True,
+                        stop=True,
+                    )
+                if half == 0:
+                    nc.scalar.copy(out=result[:, cols, :], in_=out_bank[:].rearrange("p z y -> p y z"))
+                else:
+                    nc.vector.tensor_copy(out=result[:, cols, :], in_=out_bank[:].rearrange("p z y -> p y z"))
+            nc.sync.dma_start(
+                out=out[b].rearrange("(m r) y z -> m r (y z)", r=ROWS)[:, r, :],
+                in_=result[:].rearrange("p y z -> p (y z)"),
+            )
+
+        for b in range(RAW_SLOTS):
+            load(b)
+        for step in range(-PREP_LEAD, UNITS):
+            if 0 <= step + STAGE1_LEAD - 1 < UNITS:
+                quantise_t(step + STAGE1_LEAD - 1)
+            if step + PREP_LEAD < UNITS:
+                prepare(step + PREP_LEAD)
+            if 0 <= step + STAGE1_LEAD < UNITS:
+                stage1(step + STAGE1_LEAD)
+            if step >= 0:
+                stage2(step)

@@ -66,40 +66,51 @@ def tile_span2oscorer_pa_t_kernel(tc, xp, yp, w, out):
                     )
             nc.sync.dma_start(out=y_raw[:, slot, :, 0 : K - 1], in_=yp[b].rearrange("(r m) k -> m r k", r=ROWS))
 
-        def prepare(piece):
-            b, quarter = divmod(piece, ROWS)
-            slot, parity = b % RAW_SLOTS, b % 2
-            first, half = divmod(quarter, 2)
-            cols = slice(half * HALF, (half + 1) * HALF)
+        xy_grouped = {}
+        w_grouped = {}
 
-            raw, codes, scales = ((x_raw, x_codes, x_scales), (y_raw, y_codes, y_scales))[first]
-            words = raw[:, slot].bitcast(F32)
+        def regroup(piece):
+            part, half = divmod(piece, 2)
+            b, first = divmod(part, 2)
+            slot = b % RAW_SLOTS
+            if half == 0:
+                xy_grouped[part] = grouped.tile([P, ROWS, P, PACK], BF16, align_bytes=64, name="xy_grouped")
+                w_grouped[part] = grouped.tile([P, PACK, P, PACK], BF16, align_bytes=64, name="w_grouped")
+
+            qs = slice(half * (P // 2), (half + 1) * (P // 2))
+            nc.vector.tensor_copy(
+                out=w_grouped[part][:].rearrange("p f q t -> p q t f")[:, qs],
+                in_=w_raw[:, slot, first].rearrange("p t (q f) -> p q t f", f=PACK)[:, qs],
+            )
+
+            words = (x_raw, y_raw)[first][:, slot].bitcast(F32)
             flipped = flip_banks.tile([P, 2, 2, P], F32)
             for pair_row in range(2):
                 for u in range(2):
-                    nc.tensor.transpose(
-                        flipped[:, pair_row, u, :], words[:, 2 * half + pair_row, u::2], identity[:]
-                    )
-            xy_grouped = grouped.tile([P, 2, P, PACK], BF16, align_bytes=64)
-            nc.scalar.copy(out=xy_grouped[:].bitcast(F32), in_=flipped[:].rearrange("p r u m -> p r m u"))
-
-            w_grouped = grouped.tile([P, 2, P, PACK], BF16, align_bytes=64)
-            nc.vector.tensor_copy(
-                out=w_grouped[:],
-                in_=w_raw[:, slot, first].rearrange("p t (q f) -> p f q t", f=PACK)[:, 2 * half : 2 * half + 2],
+                    nc.tensor.transpose(flipped[:, pair_row, u, :], words[:, 2 * half + pair_row, u::2], identity[:])
+            nc.scalar.copy(
+                out=xy_grouped[part][:, 2 * half : 2 * half + 2].rearrange("p r m t -> p (r m t)").bitcast(F32),
+                in_=flipped[:].rearrange("p r u m -> p r m u"),
             )
-            nc.vector.quantize_mx(
-                out=codes[:, parity, cols].bitcast(FP8X4),
-                scales=scales[:, parity, cols],
-                in_=xy_grouped[:].rearrange("p r m t -> p (r m t)"),
-            )
-            nc.vector.quantize_mx(
-                out=w_codes[:, parity, first, cols].bitcast(FP8X4),
-                scales=w_scales[:, parity, first, cols],
-                in_=w_grouped[:].rearrange("p f q t -> p (f q t)"),
-            )
-            if quarter == ROWS - 1 and b + RAW_SLOTS < B:
+            if first == 1 and half == 1 and b + RAW_SLOTS < B:
                 load(b + RAW_SLOTS)
+
+        def quantise_xy(part):
+            b, first = divmod(part, 2)
+            codes, scales = ((x_codes, x_scales), (y_codes, y_scales))[first]
+            nc.vector.quantize_mx(
+                out=codes[:, b % 2].bitcast(FP8X4),
+                scales=scales[:, b % 2],
+                in_=xy_grouped[part][:].rearrange("p r m t -> p (r m t)"),
+            )
+
+        def quantise_w(part):
+            b, z = divmod(part, 2)
+            nc.vector.quantize_mx(
+                out=w_codes[:, b % 2, z].bitcast(FP8X4),
+                scales=w_scales[:, b % 2, z],
+                in_=w_grouped[part][:].rearrange("p f q t -> p (f q t)"),
+            )
 
         t_grouped = {}
         t_quantised = {}
@@ -162,10 +173,15 @@ def tile_span2oscorer_pa_t_kernel(tc, xp, yp, w, out):
         for b in range(RAW_SLOTS):
             load(b)
         for step in range(-PREP_LEAD, UNITS):
+            piece = step + PREP_LEAD
+            if piece < UNITS:
+                regroup(piece)
             if 0 <= step + STAGE1_LEAD - 1 < UNITS:
                 quantise_t(step + STAGE1_LEAD - 1)
-            if step + PREP_LEAD < UNITS:
-                prepare(step + PREP_LEAD)
+            if piece <= UNITS and piece % 2 == 0 and piece > 0:
+                quantise_xy(piece // 2 - 1)
+            if piece < UNITS and piece % 2 == 1:
+                quantise_w(piece // 2)
             if 0 <= step + STAGE1_LEAD < UNITS:
                 stage1(step + STAGE1_LEAD)
             if step >= 0:

@@ -115,7 +115,7 @@ def tile_span2oscorer_pa_t_kernel(tc, xp, yp, w, out):
         t_grouped = {}
         t_quantised = {}
 
-        def stage1(unit):
+        def stage1(unit, share):
             b, r = divmod(unit, ROWS)
             parity = b % 2
             t_grouped[unit] = grouped.tile([P, Z, P, PACK], BF16, align_bytes=64, name="t_grouped")
@@ -131,7 +131,8 @@ def tile_span2oscorer_pa_t_kernel(tc, xp, yp, w, out):
                         start=True,
                         stop=True,
                     )
-                nc.scalar.copy(out=t_grouped[unit][:, z], in_=t_bank[:].rearrange("p t m -> p m t"))
+                copy = nc.vector.tensor_copy if share and z == 1 else nc.scalar.copy
+                copy(out=t_grouped[unit][:, z], in_=t_bank[:].rearrange("p t m -> p m t"))
 
         def quantise_t(unit):
             t_codes = grouped.tile([P, Z * P], U32, align_bytes=64)
@@ -183,6 +184,6 @@ def tile_span2oscorer_pa_t_kernel(tc, xp, yp, w, out):
             if piece < UNITS and piece % 2 == 1:
                 quantise_w(piece // 2)
             if 0 <= step + STAGE1_LEAD < UNITS:
-                stage1(step + STAGE1_LEAD)
+                stage1(step + STAGE1_LEAD, piece >= UNITS)
             if step >= 0:
                 stage2(step)

@@ -68,6 +68,7 @@ def tile_span2oscorer_pa_t_kernel(tc, xp, yp, w, out):
 
         xy_grouped = {}
         w_grouped = {}
+        flipped = {}
 
         def regroup(piece):
             part, half = divmod(piece, 2)
@@ -84,13 +85,17 @@ def tile_span2oscorer_pa_t_kernel(tc, xp, yp, w, out):
             )
 
             words = (x_raw, y_raw)[first][:, slot].bitcast(F32)
-            flipped = flip_banks.tile([P, 2, 2, P], F32)
-            for pair_row in range(2):
-                for u in range(2):
-                    nc.tensor.transpose(flipped[:, pair_row, u, :], words[:, 2 * half + pair_row, u::2], identity[:])
+            if half == 0:
+                for pair in range(2):
+                    flipped[pair] = flip_banks.tile([P, 2, 2, P], F32, name="flipped")
+                    for pair_row in range(2):
+                        for u in range(2):
+                            nc.tensor.transpose(
+                                flipped[pair][:, pair_row, u, :], words[:, 2 * pair + pair_row, u::2], identity[:]
+                            )
             nc.scalar.copy(
                 out=xy_grouped[part][:, 2 * half : 2 * half + 2].rearrange("p r m t -> p (r m t)").bitcast(F32),
-                in_=flipped[:].rearrange("p r u m -> p r m u"),
+                in_=flipped[half][:].rearrange("p r u m -> p r m u"),
             )
             if first == 1 and half == 1 and b + RAW_SLOTS < B:
                 load(b + RAW_SLOTS)

@@ -70,35 +70,36 @@ def tile_span2oscorer_pa_t_kernel(tc, xp, yp, w, out):
         w_grouped = {}
         flipped = {}
 
-        def regroup(piece):
+        def regroup_w(piece):
             part, half = divmod(piece, 2)
-            b, first = divmod(part, 2)
-            slot = b % RAW_SLOTS
+            b, z = divmod(part, 2)
             if half == 0:
-                xy_grouped[part] = grouped.tile([P, ROWS, P, PACK], BF16, align_bytes=64, name="xy_grouped")
                 w_grouped[part] = grouped.tile([P, PACK, P, PACK], BF16, align_bytes=64, name="w_grouped")
-
-            qs = slice(half * (P // 2), (half + 1) * (P // 2))
+            hs = slice(half * (P // 4), (half + 1) * (P // 4))
             nc.vector.tensor_copy(
-                out=w_grouped[part][:].rearrange("p f q t -> p q t f")[:, qs],
-                in_=w_raw[:, slot, first].rearrange("p t (q f) -> p q t f", f=PACK)[:, qs],
+                out=w_grouped[part][:].rearrange("p f (h q) t -> p h t q f", q=2)[:, hs],
+                in_=w_raw[:, b % RAW_SLOTS, z].rearrange("p t (h q f) -> p h t q f", q=2, f=PACK)[:, hs],
             )
 
-            words = (x_raw, y_raw)[first][:, slot].bitcast(F32)
+        def flip(part):
+            b, first = divmod(part, 2)
+            words = (x_raw, y_raw)[first][:, b % RAW_SLOTS].bitcast(F32)
+            for pair in range(2):
+                flipped[pair] = flip_banks.tile([P, 2, 2, P], F32, name="flipped")
+                for pair_row in range(2):
+                    for u in range(2):
+                        nc.tensor.transpose(
+                            flipped[pair][:, pair_row, u, :], words[:, 2 * pair + pair_row, u::2], identity[:]
+                        )
+
+        def regroup_xy(piece):
+            part, half = divmod(piece, 2)
             if half == 0:
-                for pair in range(2):
-                    flipped[pair] = flip_banks.tile([P, 2, 2, P], F32, name="flipped")
-                    for pair_row in range(2):
-                        for u in range(2):
-                            nc.tensor.transpose(
-                                flipped[pair][:, pair_row, u, :], words[:, 2 * pair + pair_row, u::2], identity[:]
-                            )
+                xy_grouped[part] = grouped.tile([P, ROWS, P, PACK], BF16, align_bytes=64, name="xy_grouped")
             nc.scalar.copy(
                 out=xy_grouped[part][:, 2 * half : 2 * half + 2].rearrange("p r m t -> p (r m t)").bitcast(F32),
                 in_=flipped[half][:].rearrange("p r u m -> p r m u"),
             )
-            if first == 1 and half == 1 and b + RAW_SLOTS < B:
-                load(b + RAW_SLOTS)
 
         def quantise_xy(part):
             b, first = divmod(part, 2)
@@ -180,15 +181,36 @@ def tile_span2oscorer_pa_t_kernel(tc, xp, yp, w, out):
             load(b)
         for step in range(-PREP_LEAD, UNITS):
             piece = step + PREP_LEAD
-            if piece < UNITS:
-                regroup(piece)
-            if 0 <= step + STAGE1_LEAD - 1 < UNITS:
-                quantise_t(step + STAGE1_LEAD - 1)
-            if piece <= UNITS and piece % 2 == 0 and piece > 0:
-                quantise_xy(piece // 2 - 1)
-            if piece < UNITS and piece % 2 == 1:
-                quantise_w(piece // 2)
-            if 0 <= step + STAGE1_LEAD < UNITS:
-                stage1(step + STAGE1_LEAD, piece >= UNITS)
+            ahead = step + STAGE1_LEAD
+            if step < 1:
+                if 0 <= step + 1:
+                    quantise_t(step + 1)
+                if ahead >= 0:
+                    stage1(ahead, False)
+                regroup_w(piece)
+                if piece % 2 == 0 and piece > 0:
+                    quantise_xy(piece // 2 - 1)
+                if piece % 2 == 1:
+                    quantise_w(piece // 2)
+                if piece % 2 == 0:
+                    flip(piece // 2)
+                regroup_xy(piece)
+            else:
+                if piece < UNITS:
+                    regroup_w(piece)
+                if step + 1 < UNITS:
+                    quantise_t(step + 1)
+                if piece <= UNITS and piece % 2 == 0:
+                    quantise_xy(piece // 2 - 1)
+                if piece < UNITS:
+                    if piece % 2 == 1:
+                        quantise_w(piece // 2)
+                    if piece % 2 == 0:
+                        flip(piece // 2)
+                    regroup_xy(piece)
+                if ahead < UNITS:
+                    stage1(ahead, piece >= UNITS)
+            if piece < UNITS and piece % ROWS == ROWS - 1 and piece // ROWS + RAW_SLOTS < B:
+                load(piece // ROWS + RAW_SLOTS)
             if step >= 0:
                 stage2(step)

@@ -40,6 +40,15 @@ def tile_span2oscorer_pa_t_kernel(tc, xp, yp, w, out):
 
         identity = fixed.tile([P, P], F32)
         make_identity(nc, identity[:])
+        zeros = fixed.tile([P, N], BF16)
+        nc.vector.memset(zeros[:], 0.0)
+
+        def keep_warm(count):
+            bank = out_banks.tile([P, Z, HALF], F32, name="out_bank")
+            for i in range(count):
+                nc.tensor.matmul(
+                    bank[:].rearrange("p z y -> p (z y)"), lhsT=zeros[:, 0:P], rhs=zeros[:], start=True, stop=True
+                )
 
         x_raw = fixed.tile([P, RAW_SLOTS, ROWS, K], BF16)
         y_raw = fixed.tile([P, RAW_SLOTS, ROWS, K], BF16)
@@ -118,27 +127,31 @@ def tile_span2oscorer_pa_t_kernel(tc, xp, yp, w, out):
                 in_=w_grouped[part][:].rearrange("p f q t -> p (f q t)"),
             )
 
+        t_of_unit = {}
         t_grouped = {}
         t_quantised = {}
 
-        def stage1(unit, share):
+        def multiply_w(unit, z):
             b, r = divmod(unit, ROWS)
             parity = b % 2
+            bank = t_banks.tile([P, PACK, P], F32, name="t_bank")
+            for t in range(PACK):
+                nc.tensor.matmul_mx(
+                    out=bank[:, t, :],
+                    lhsT=w_codes[:, parity, z, t * P : (t + 1) * P].bitcast(FP8X4),
+                    lhsT_scale=w_scales[:, parity, z, t * P : (t + 1) * P],
+                    rhs=x_codes[:, parity, r * P : (r + 1) * P].bitcast(FP8X4),
+                    rhs_scale=x_scales[:, parity, r * P : (r + 1) * P],
+                    start=True,
+                    stop=True,
+                )
+            t_of_unit[unit, z] = bank
+
+        def regroup_t(unit, share):
             t_grouped[unit] = grouped.tile([P, Z, P, PACK], BF16, align_bytes=64, name="t_grouped")
             for z in range(Z):
-                t_bank = t_banks.tile([P, PACK, P], F32)
-                for t in range(PACK):
-                    nc.tensor.matmul_mx(
-                        out=t_bank[:, t, :],
-                        lhsT=w_codes[:, parity, z, t * P : (t + 1) * P].bitcast(FP8X4),
-                        lhsT_scale=w_scales[:, parity, z, t * P : (t + 1) * P],
-                        rhs=x_codes[:, parity, r * P : (r + 1) * P].bitcast(FP8X4),
-                        rhs_scale=x_scales[:, parity, r * P : (r + 1) * P],
-                        start=True,
-                        stop=True,
-                    )
                 copy = nc.vector.tensor_copy if share and z == 1 else nc.scalar.copy
-                copy(out=t_grouped[unit][:, z], in_=t_bank[:].rearrange("p t m -> p m t"))
+                copy(out=t_grouped[unit][:, z], in_=t_of_unit[unit, z][:].rearrange("p t m -> p m t"))
 
         def quantise_t(unit):
             t_codes = grouped.tile([P, Z * P], U32, align_bytes=64)
@@ -179,6 +192,7 @@ def tile_span2oscorer_pa_t_kernel(tc, xp, yp, w, out):
 
         for b in range(RAW_SLOTS):
             load(b)
+        keep_warm(7)
         for step in range(-PREP_LEAD, UNITS):
             piece = step + PREP_LEAD
             ahead = step + STAGE1_LEAD
@@ -186,7 +200,9 @@ def tile_span2oscorer_pa_t_kernel(tc, xp, yp, w, out):
                 if 0 <= step + 1:
                     quantise_t(step + 1)
                 if ahead >= 0:
-                    stage1(ahead, False)
+                    for z in range(Z):
+                        multiply_w(ahead, z)
+                    regroup_t(ahead, False)
                 regroup_w(piece)
                 if piece % 2 == 0 and piece > 0:
                     quantise_xy(piece // 2 - 1)
@@ -202,14 +218,18 @@ def tile_span2oscorer_pa_t_kernel(tc, xp, yp, w, out):
                     quantise_t(step + 1)
                 if piece <= UNITS and piece % 2 == 0:
                     quantise_xy(piece // 2 - 1)
+                if piece < UNITS and piece % 2 == 1:
+                    quantise_w(piece // 2)
+                if ahead < UNITS:
+                    multiply_w(ahead, 0)
+                if piece < UNITS and piece % 2 == 0:
+                    flip(piece // 2)
+                if ahead < UNITS:
+                    multiply_w(ahead, 1)
                 if piece < UNITS:
-                    if piece % 2 == 1:
-                        quantise_w(piece // 2)
-                    if piece % 2 == 0:
-                        flip(piece // 2)
                     regroup_xy(piece)
                 if ahead < UNITS:
-                    stage1(ahead, piece >= UNITS)
+                    regroup_t(ahead, UNITS - ROWS <= ahead < UNITS - 2)
             if piece < UNITS and piece % ROWS == ROWS - 1 and piece // ROWS + RAW_SLOTS < B:
                 load(piece // ROWS + RAW_SLOTS)
             if step >= 0:

@@ -79,12 +79,11 @@ def tile_span2oscorer_pa_t_kernel(tc, xp, yp, w, out):
         w_grouped = {}
         flipped = {}
 
-        def regroup_w(piece):
-            part, half = divmod(piece, 2)
+        def regroup_w(part, lo=0, hi=P):
             b, z = divmod(part, 2)
-            if half == 0:
+            if lo == 0:
                 w_grouped[part] = grouped.tile([P, PACK, P, PACK], BF16, align_bytes=64, name="w_grouped")
-            hs = slice(half * (P // 4), (half + 1) * (P // 4))
+            hs = slice(lo // 2, hi // 2)
             nc.vector.tensor_copy(
                 out=w_grouped[part][:].rearrange("p f (h q) t -> p h t q f", q=2)[:, hs],
                 in_=w_raw[:, b % RAW_SLOTS, z].rearrange("p t (h q f) -> p h t q f", q=2, f=PACK)[:, hs],
@@ -110,13 +109,14 @@ def tile_span2oscorer_pa_t_kernel(tc, xp, yp, w, out):
                 in_=flipped[half][:].rearrange("p r u m -> p r m u"),
             )
 
-        def quantise_xy(part):
+        def quantise_xy(part, rows=slice(0, ROWS)):
             b, first = divmod(part, 2)
             codes, scales = ((x_codes, x_scales), (y_codes, y_scales))[first]
+            cols = slice(rows.start * P, rows.stop * P)
             nc.vector.quantize_mx(
-                out=codes[:, b % 2].bitcast(FP8X4),
-                scales=scales[:, b % 2],
-                in_=xy_grouped[part][:].rearrange("p r m t -> p (r m t)"),
+                out=codes[:, b % 2, cols].bitcast(FP8X4),
+                scales=scales[:, b % 2, cols],
+                in_=xy_grouped[part][:, rows].rearrange("p r m t -> p (r m t)"),
             )
 
         def quantise_w(part):
@@ -147,11 +147,10 @@ def tile_span2oscorer_pa_t_kernel(tc, xp, yp, w, out):
                 )
             t_of_unit[unit, z] = bank
 
-        def regroup_t(unit, share):
-            t_grouped[unit] = grouped.tile([P, Z, P, PACK], BF16, align_bytes=64, name="t_grouped")
-            for z in range(Z):
-                copy = nc.vector.tensor_copy if share and z == 1 else nc.scalar.copy
-                copy(out=t_grouped[unit][:, z], in_=t_of_unit[unit, z][:].rearrange("p t m -> p m t"))
+        def regroup_t(unit, z, copy):
+            if z == 0:
+                t_grouped[unit] = grouped.tile([P, Z, P, PACK], BF16, align_bytes=64, name="t_grouped")
+            copy(out=t_grouped[unit][:, z], in_=t_of_unit[unit, z][:].rearrange("p t m -> p m t"))
 
         def quantise_t(unit):
             t_codes = grouped.tile([P, Z * P], U32, align_bytes=64)
@@ -190,47 +189,72 @@ def tile_span2oscorer_pa_t_kernel(tc, xp, yp, w, out):
                 in_=result[:].rearrange("p y z -> p (y z)"),
             )
 
+        S, V = nc.scalar.copy, nc.vector.tensor_copy
         for b in range(RAW_SLOTS):
             load(b)
         keep_warm(7)
-        for step in range(-PREP_LEAD, UNITS):
+        regroup_w(0, 0, P // 2)
+        regroup_w(0, P // 2, P)
+        flip(0)
+        regroup_xy(0)
+        regroup_xy(1)
+        quantise_w(0)
+        regroup_w(1, 0, P // 2)
+        quantise_xy(0, slice(0, 2))
+        multiply_w(0, 0)
+        multiply_w(1, 0)
+        regroup_t(0, 0, S)
+        regroup_t(1, 0, S)
+        regroup_w(1, P // 2, P)
+        quantise_xy(0, slice(2, 4))
+        flip(1)
+        regroup_xy(2)
+        regroup_xy(3)
+        quantise_w(1)
+        multiply_w(0, 1)
+        regroup_t(0, 1, S)
+        multiply_w(1, 1)
+        regroup_t(1, 1, S)
+        regroup_w(2)
+        quantise_xy(1)
+        quantise_t(0)
+        multiply_w(2, 0)
+        regroup_t(2, 0, S)
+        multiply_w(2, 1)
+        regroup_t(2, 1, S)
+        quantise_w(2)
+        quantise_t(1)
+        flip(2)
+        regroup_xy(4)
+        regroup_xy(5)
+        load(4)
+        regroup_w(3)
+        stage2(0)
+        flip(3)
+        quantise_xy(2)
+        regroup_xy(6)
+        for step in range(1, UNITS):
             piece = step + PREP_LEAD
             ahead = step + STAGE1_LEAD
-            if step < 1:
-                if 0 <= step + 1:
-                    quantise_t(step + 1)
-                if ahead >= 0:
-                    for z in range(Z):
-                        multiply_w(ahead, z)
-                    regroup_t(ahead, False)
-                regroup_w(piece)
-                if piece % 2 == 0 and piece > 0:
-                    quantise_xy(piece // 2 - 1)
-                if piece % 2 == 1:
-                    quantise_w(piece // 2)
-                if piece % 2 == 0:
-                    flip(piece // 2)
+            if piece < UNITS and piece % 2 == 0:
+                regroup_w(piece // 2)
+            if step + 1 < UNITS:
+                quantise_t(step + 1)
+            if piece <= UNITS and piece % 2 == 0:
+                quantise_xy(piece // 2 - 1)
+            if piece < UNITS and piece % 2 == 1:
+                quantise_w(piece // 2)
+            if ahead < UNITS:
+                multiply_w(ahead, 0)
+            if piece < UNITS and piece % 2 == 0:
+                flip(piece // 2)
+            if ahead < UNITS:
+                multiply_w(ahead, 1)
+            if piece < UNITS:
                 regroup_xy(piece)
-            else:
-                if piece < UNITS:
-                    regroup_w(piece)
-                if step + 1 < UNITS:
-                    quantise_t(step + 1)
-                if piece <= UNITS and piece % 2 == 0:
-                    quantise_xy(piece // 2 - 1)
-                if piece < UNITS and piece % 2 == 1:
-                    quantise_w(piece // 2)
-                if ahead < UNITS:
-                    multiply_w(ahead, 0)
-                if piece < UNITS and piece % 2 == 0:
-                    flip(piece // 2)
-                if ahead < UNITS:
-                    multiply_w(ahead, 1)
-                if piece < UNITS:
-                    regroup_xy(piece)
-                if ahead < UNITS:
-                    regroup_t(ahead, UNITS - ROWS <= ahead < UNITS - 2)
+            if ahead < UNITS:
+                regroup_t(ahead, 0, S)
+                regroup_t(ahead, 1, V if UNITS - ROWS <= ahead < UNITS - 2 or ahead == 16 else S)
             if piece < UNITS and piece % ROWS == ROWS - 1 and piece // ROWS + RAW_SLOTS < B:
                 load(piece // ROWS + RAW_SLOTS)
-            if step >= 0:
-                stage2(step)
+            stage2(step)

@@ -71,7 +71,7 @@ def tile_span2oscorer_pa_t_kernel(tc, xp, yp, w, out):
                 )
                 if z == 0:
                     nc.sync.dma_start(
-                        out=x_raw[:, slot, :, 0 : K - 1], in_=xp[b].rearrange("(m r) k -> m r k", r=ROWS)
+                        out=x_raw[:, slot, :, 0 : K - 1], in_=xp[b].rearrange("(r m) k -> m r k", r=ROWS)
                     )
             nc.sync.dma_start(out=y_raw[:, slot, :, 0 : K - 1], in_=yp[b].rearrange("(r m) k -> m r k", r=ROWS))
 
@@ -185,7 +185,7 @@ def tile_span2oscorer_pa_t_kernel(tc, xp, yp, w, out):
                 else:
                     nc.vector.tensor_copy(out=result[:, cols, :], in_=out_bank[:].rearrange("p z y -> p y z"))
             nc.sync.dma_start(
-                out=out[b].rearrange("(m r) y z -> m r (y z)", r=ROWS)[:, r, :],
+                out=out[b].rearrange("(r m) y z -> m r (y z)", r=ROWS)[:, r, :],
                 in_=result[:].rearrange("p y z -> p (y z)"),
             )
 

from contextlib import ExitStack

import concourse.mybir as mybir
from concourse.masks import make_identity

BF16 = mybir.dt.bfloat16
F32 = mybir.dt.float32
U32 = mybir.dt.uint32
U8 = mybir.dt.uint8
FP8X4 = mybir.dt.float8_e4m3fn_x4

B = 8
Z = 2
N = 512
K = 512
P = 128
PACK = 4
ROWS = N // P
HALF = N // 2

UNITS = B * ROWS
RAW_SLOTS = 4
RESULT_SLOTS = 16
PREP_LEAD = 6
STAGE1_LEAD = 2

FLOPS = 2 * 2 * B * Z * N * K * K


def tile_span2oscorer_pa_t_kernel(tc, xp, yp, w, out):
    nc = tc.nc
    with ExitStack() as stack:
        fixed = stack.enter_context(tc.tile_pool(name="fixed", bufs=1))
        grouped = stack.enter_context(tc.tile_pool(name="grouped", bufs=3))
        results = stack.enter_context(tc.tile_pool(name="results", bufs=RESULT_SLOTS))
        flip_banks = stack.enter_context(tc.psum_pool(name="flip_banks", bufs=2))
        t_banks = stack.enter_context(tc.psum_pool(name="t_banks", bufs=3))
        out_banks = stack.enter_context(tc.psum_pool(name="out_banks", bufs=3))
        stack.enter_context(tc.manual_schedule())

        identity = fixed.tile([P, P], F32)
        make_identity(nc, identity[:])
        zeros = fixed.tile([P, N], BF16)
        nc.vector.memset(zeros[:], 0.0)

        def keep_warm(count):
            bank = out_banks.tile([P, Z, HALF], F32, name="out_bank")
            for i in range(count):
                nc.tensor.matmul(
                    bank[:].rearrange("p z y -> p (z y)"), lhsT=zeros[:, 0:P], rhs=zeros[:], start=True, stop=True
                )

        x_raw = fixed.tile([P, RAW_SLOTS, ROWS, K], BF16)
        y_raw = fixed.tile([P, RAW_SLOTS, ROWS, K], BF16)
        w_raw = fixed.tile([P, RAW_SLOTS, Z, PACK, K], BF16)
        nc.vector.memset(x_raw[:, :, :, K - 16 : K], 1.0)
        nc.vector.memset(y_raw[:, :, :, K - 16 : K], 1.0)

        x_codes = fixed.tile([P, 2, N], U32, align_bytes=64)
        x_scales = fixed.tile([P, 2, N], U8, align_bytes=64)
        y_codes = fixed.tile([P, 2, N], U32, align_bytes=64)
        y_scales = fixed.tile([P, 2, N], U8, align_bytes=64)
        w_codes = fixed.tile([P, 2, Z, K], U32, align_bytes=64)
        w_scales = fixed.tile([P, 2, Z, K], U8, align_bytes=64)

        def load(b):
            slot = b % RAW_SLOTS
            for z in range(Z):
                nc.sync.dma_start(
                    out=w_raw[:, slot, z], in_=w[b, z].rearrange("(p t) j -> p t j", t=PACK)
                )
                if z == 0:
                    nc.sync.dma_start(
                        out=x_raw[:, slot, :, 0 : K - 1], in_=xp[b].rearrange("(r m) k -> m r k", r=ROWS)
                    )
            nc.sync.dma_start(out=y_raw[:, slot, :, 0 : K - 1], in_=yp[b].rearrange("(r m) k -> m r k", r=ROWS))

        xy_grouped = {}
        w_grouped = {}
        flipped = {}

        def regroup_w(part, lo=0, hi=P):
            b, z = divmod(part, 2)
            if lo == 0:
                w_grouped[part] = grouped.tile([P, PACK, P, PACK], BF16, align_bytes=64, name="w_grouped")
            hs = slice(lo // 2, hi // 2)
            nc.vector.tensor_copy(
                out=w_grouped[part][:].rearrange("p f (h q) t -> p h t q f", q=2)[:, hs],
                in_=w_raw[:, b % RAW_SLOTS, z].rearrange("p t (h q f) -> p h t q f", q=2, f=PACK)[:, hs],
            )

        def flip(part):
            b, first = divmod(part, 2)
            words = (x_raw, y_raw)[first][:, b % RAW_SLOTS].bitcast(F32)
            for pair in range(2):
                flipped[pair] = flip_banks.tile([P, 2, 2, P], F32, name="flipped")
                for pair_row in range(2):
                    for u in range(2):
                        nc.tensor.transpose(
                            flipped[pair][:, pair_row, u, :], words[:, 2 * pair + pair_row, u::2], identity[:]
                        )

        def regroup_xy(piece):
            part, half = divmod(piece, 2)
            if half == 0:
                xy_grouped[part] = grouped.tile([P, ROWS, P, PACK], BF16, align_bytes=64, name="xy_grouped")
            nc.scalar.copy(
                out=xy_grouped[part][:, 2 * half : 2 * half + 2].rearrange("p r m t -> p (r m t)").bitcast(F32),
                in_=flipped[half][:].rearrange("p r u m -> p r m u"),
            )

        def quantise_xy(part, rows=slice(0, ROWS)):
            b, first = divmod(part, 2)
            codes, scales = ((x_codes, x_scales), (y_codes, y_scales))[first]
            cols = slice(rows.start * P, rows.stop * P)
            nc.vector.quantize_mx(
                out=codes[:, b % 2, cols].bitcast(FP8X4),
                scales=scales[:, b % 2, cols],
                in_=xy_grouped[part][:, rows].rearrange("p r m t -> p (r m t)"),
            )

        def quantise_w(part):
            b, z = divmod(part, 2)
            nc.vector.quantize_mx(
                out=w_codes[:, b % 2, z].bitcast(FP8X4),
                scales=w_scales[:, b % 2, z],
                in_=w_grouped[part][:].rearrange("p f q t -> p (f q t)"),
            )

        t_of_unit = {}
        t_grouped = {}
        t_quantised = {}

        def multiply_w(unit, z):
            b, r = divmod(unit, ROWS)
            parity = b % 2
            bank = t_banks.tile([P, PACK, P], F32, name="t_bank")
            for t in range(PACK):
                nc.tensor.matmul_mx(
                    out=bank[:, t, :],
                    lhsT=w_codes[:, parity, z, t * P : (t + 1) * P].bitcast(FP8X4),
                    lhsT_scale=w_scales[:, parity, z, t * P : (t + 1) * P],
                    rhs=x_codes[:, parity, r * P : (r + 1) * P].bitcast(FP8X4),
                    rhs_scale=x_scales[:, parity, r * P : (r + 1) * P],
                    start=True,
                    stop=True,
                )
            t_of_unit[unit, z] = bank

        def regroup_t(unit, z, copy):
            if z == 0:
                t_grouped[unit] = grouped.tile([P, Z, P, PACK], BF16, align_bytes=64, name="t_grouped")
            copy(out=t_grouped[unit][:, z], in_=t_of_unit[unit, z][:].rearrange("p t m -> p m t"))

        def quantise_t(unit):
            t_codes = grouped.tile([P, Z * P], U32, align_bytes=64)
            t_scales = grouped.tile([P, Z * P], U8, align_bytes=64)
            nc.vector.quantize_mx(
                out=t_codes[:].bitcast(FP8X4),
                scales=t_scales[:],
                in_=t_grouped[unit][:].rearrange("p z m t -> p (z m t)"),
            )
            t_quantised[unit] = (t_codes, t_scales)

        def stage2(unit):
            b, r = divmod(unit, ROWS)
            parity = b % 2
            t_codes, t_scales = t_quantised[unit]
            result = results.tile([P, N, Z], F32)
            for half in range(2):
                cols = slice(half * HALF, (half + 1) * HALF)
                out_bank = out_banks.tile([P, Z, HALF], F32)
                for z in range(Z):
                    nc.tensor.matmul_mx(
                        out=out_bank[:, z, :],
                        lhsT=t_codes[:, z * P : (z + 1) * P].bitcast(FP8X4),
                        lhsT_scale=t_scales[:, z * P : (z + 1) * P],
                        rhs=y_codes[:, parity, cols].bitcast(FP8X4),
                        rhs_scale=y_scales[:, parity, cols],
                        start=True,
                        stop=True,
                    )
                if half == 0:
                    nc.scalar.copy(out=result[:, cols, :], in_=out_bank[:].rearrange("p z y -> p y z"))
                else:
                    nc.vector.tensor_copy(out=result[:, cols, :], in_=out_bank[:].rearrange("p z y -> p y z"))
            nc.sync.dma_start(
                out=out[b].rearrange("(r m) y z -> m r (y z)", r=ROWS)[:, r, :],
                in_=result[:].rearrange("p y z -> p (y z)"),
            )

        S, V = nc.scalar.copy, nc.vector.tensor_copy
        for b in range(RAW_SLOTS):
            load(b)
        keep_warm(7)
        regroup_w(0, 0, P // 2)
        regroup_w(0, P // 2, P)
        flip(0)
        regroup_xy(0)
        regroup_xy(1)
        quantise_w(0)
        regroup_w(1, 0, P // 2)
        quantise_xy(0, slice(0, 2))
        multiply_w(0, 0)
        multiply_w(1, 0)
        regroup_t(0, 0, S)
        regroup_t(1, 0, S)
        regroup_w(1, P // 2, P)
        quantise_xy(0, slice(2, 4))
        flip(1)
        regroup_xy(2)
        regroup_xy(3)
        quantise_w(1)
        multiply_w(0, 1)
        regroup_t(0, 1, S)
        multiply_w(1, 1)
        regroup_t(1, 1, S)
        regroup_w(2)
        quantise_xy(1)
        quantise_t(0)
        multiply_w(2, 0)
        regroup_t(2, 0, S)
        multiply_w(2, 1)
        regroup_t(2, 1, S)
        quantise_w(2)
        quantise_t(1)
        flip(2)
        regroup_xy(4)
        regroup_xy(5)
        load(4)
        regroup_w(3)
        stage2(0)
        flip(3)
        quantise_xy(2)
        regroup_xy(6)
        for step in range(1, UNITS):
            piece = step + PREP_LEAD
            ahead = step + STAGE1_LEAD
            if piece < UNITS and piece % 2 == 0:
                regroup_w(piece // 2)
            if step + 1 < UNITS:
                quantise_t(step + 1)
            if piece <= UNITS and piece % 2 == 0:
                quantise_xy(piece // 2 - 1)
            if piece < UNITS and piece % 2 == 1:
                quantise_w(piece // 2)
            if ahead < UNITS:
                multiply_w(ahead, 0)
            if piece < UNITS and piece % 2 == 0:
                flip(piece // 2)
            if ahead < UNITS:
                multiply_w(ahead, 1)
            if piece < UNITS:
                regroup_xy(piece)
            if ahead < UNITS:
                regroup_t(ahead, 0, S)
                regroup_t(ahead, 1, V if UNITS - ROWS <= ahead < UNITS - 2 or ahead == 16 else S)
            if piece < UNITS and piece % ROWS == ROWS - 1 and piece // ROWS + RAW_SLOTS < B:
                load(piece // ROWS + RAW_SLOTS)
            stage2(step)
